import numpy as np
import ml_dtypes


def mxq(x, axis, fmt="e4m3"):
    dtype, down = {"e4m3": (ml_dtypes.float8_e4m3fn, 7), "e5m2": (ml_dtypes.float8_e5m2, 14)}[fmt]
    v = np.moveaxis(np.asarray(x, np.float32).astype(ml_dtypes.bfloat16).astype(np.float64), axis, -1)
    blocks = v.reshape(v.shape[:-1] + (-1, 32))
    amax = np.abs(blocks).max(-1, keepdims=True)
    byte = np.maximum(np.where(amax > 0, np.frexp(amax)[1] - 1 + 127, 0) - down, 1)
    scale = np.exp2(byte - 127.0)
    codes = (blocks / scale).astype(np.float32).astype(dtype).astype(np.float64)
    return np.moveaxis((codes * scale).reshape(v.shape), -1, axis)


WIDE = False


def mx_kscale(k):
    if not WIDE:
        return np.ones(k)
    levels = np.array([10, -10, 5, -5, 0])
    a = np.random.permutation(np.resize(levels, k // 512 * 4)).reshape(k // 512, 4)
    idx = np.arange(k)
    return np.exp2(a[idx // 512, idx % 128 // 32])


BF16 = ml_dtypes.bfloat16


def bf(x):
    return np.asarray(x, np.float32).astype(BF16)


def f64(x):
    return np.asarray(x).astype(np.float64)


E2M1 = np.array([0.0, 0.5, 1.0, 1.5, 2.0, 3.0, 4.0, 6.0, -0.0, -0.5, -1.0, -1.5, -2.0, -3.0, -4.0, -6.0])


def pack_weight(w, fmt):
    k, n = w.shape
    w = f64(bf(w)).reshape(k // 32, 32, n)
    amax = np.abs(w).max(1)
    if fmt == "e4m3":
        byte = np.frexp(amax)[1] - 1 + 127 - 7
    else:
        mant, ex = np.frexp(amax / 6.0)
        byte = np.where(mant > 0.5, ex, ex - 1) + 127
    byte = np.clip(np.where(amax > 0, byte, 1), 1, 254)
    scaled = (w * np.exp2(127.0 - byte)[:, None, :]).reshape(k, n).astype(np.float32)
    by_word = np.ascontiguousarray(scaled.reshape(k // 512, 128, 4, n).transpose(0, 1, 3, 2))
    if fmt == "e4m3":
        words = by_word.astype(ml_dtypes.float8_e4m3fn).view(np.uint8)
    else:
        c = by_word.astype(ml_dtypes.float4_e2m1fn).view(np.uint8) & 0xF
        words = c[..., 0::2] | (c[..., 1::2] << 4)
    return np.ascontiguousarray(words), np.ascontiguousarray(byte.astype(np.uint8).reshape(k // 512, 16, n))


def unpack_weight(words, scales, fmt):
    g, p, n, _ = words.shape
    if fmt == "e4m3":
        vals = np.ascontiguousarray(words).view(ml_dtypes.float8_e4m3fn).astype(np.float64)
    else:
        nib = np.empty((g, p, n, 4), np.uint8)
        nib[..., 0::2] = words & 0xF
        nib[..., 1::2] = words >> 4
        vals = E2M1[nib]
    vals = vals * np.repeat(np.exp2(scales.astype(np.float64) - 127.0), 8, axis=1)[..., None]
    return vals.transpose(0, 1, 3, 2).reshape(g * 512, n)

def pack4(w):
    words, scales = pack_weight(w, "e2m1")
    return words.reshape(words.shape[0], 128, -1), scales


def unpack4(words, scales):
    return unpack_weight(words.reshape(words.shape[0], 128, -1, 2), scales, "e2m1")


B, S, D_MODEL, N_HEADS, QK_ROPE, QK_NOPE, KV_LORA, V_DIM = 2, 64, 8192, 16, 128, 128, 512, 128
QK_DIM = QK_ROPE + QK_NOPE
ROPE_BASE = 10000.0


def apply_rope(r):
    freqs = 1.0 / (ROPE_BASE ** (np.arange(0, QK_ROPE, 2) / QK_ROPE))
    t = np.arange(S)[:, None] * freqs[None, :]
    cos = np.cos(t)[None, :, None, :]
    sin = np.sin(t)[None, :, None, :]
    r1 = r[..., 0::2]
    r2 = r[..., 1::2]
    return np.stack([r1 * cos - r2 * sin, r2 * cos + r1 * sin], axis=-1).reshape(r.shape)


def setup_inputs():
    s = mx_kscale(D_MODEL)
    x = bf(np.random.standard_normal((B, S, D_MODEL)) * s)
    words, scales = pack4(np.random.standard_normal((D_MODEL, N_HEADS * QK_DIM)) / np.sqrt(D_MODEL) / s[:, None])
    return {"x": x, "Wq_words": words, "Wq_scales": scales}


def reference(x, Wq_words, Wq_scales):
    q = (mxq(f64(x), 2, "e4m3") @ unpack4(Wq_words, Wq_scales)).reshape(B, S, N_HEADS, QK_DIM)
    q_nope, q_rope = q[..., :QK_NOPE], q[..., QK_NOPE:]
    return np.concatenate([q_nope, apply_rope(q_rope)], axis=-1)

@@ -1,0 +1,265 @@
+import math
+from contextlib import ExitStack
+
+import concourse.mybir as mybir
+from concourse.masks import make_identity
+
+F32 = mybir.dt.float32
+BF16 = mybir.dt.bfloat16
+I32 = mybir.dt.int32
+U32 = mybir.dt.uint32
+U8 = mybir.dt.uint8
+FP8X4 = mybir.dt.float8_e4m3fn_x4
+FP4X4 = mybir.dt.float4_e2m1fn_x4
+ALU = mybir.AluOpType
+ACT = mybir.ActivationFunctionType
+
+P = 128
+BATCH = 2
+SEQ = 64
+TOKENS = BATCH * SEQ
+D_MODEL = 8192
+HEADS = 16
+HEAD_DIM = 256
+NOPE_DIM = 128
+N_OUT = HEADS * HEAD_DIM
+PAIRS = (HEAD_DIM - NOPE_DIM) // 2
+ROPE_BASE = 10000.0
+
+PACK = 4
+K_GROUP = P * PACK
+GROUPS = D_MODEL // K_GROUP
+SCALE_ROWS = K_GROUP // 32
+BANK_COLS = 512
+BANKS = N_OUT // BANK_COLS
+HEADS_PER_BANK = BANK_COLS // HEAD_DIM
+BANK_W_BYTES = BANK_COLS * 2
+GROUP_W_BYTES = N_OUT * 2
+
+X_LOADS = 4
+GROUPS_PER_BANK = 2
+
+STRETCH = 16
+GROUPS_PER_SCALE_DMA = 4
+
+TAPER_GROUPS = 4
+PIECE_BANKS = 2
+MAIN_GROUPS = GROUPS - TAPER_GROUPS
+PIECES = BANKS // PIECE_BANKS
+W_TILES = MAIN_GROUPS + PIECES
+assert TAPER_GROUPS * PIECE_BANKS * BANK_W_BYTES == GROUP_W_BYTES
+assert STRETCH % TAPER_GROUPS == 0
+
+W_BUFS = 8
+LOOKAHEAD = W_BUFS - 1
+assert LOOKAHEAD >= PIECES
+
+TWO_PI = 2.0 * math.pi
+TWO_PI_HIGH = 6.28125
+TWO_PI_MIDDLE = math.floor((TWO_PI - TWO_PI_HIGH) * 2.0**21) / 2.0**21
+TWO_PI_LOW = TWO_PI - TWO_PI_HIGH - TWO_PI_MIDDLE
+ROUND_MAGIC = 1.5 * 2.0**23
+
+FLOPS = 2 * TOKENS * D_MODEL * N_OUT
+
+
+def build_rope_tables(nc, pool):
+    pair_index_int = pool.tile([P, PAIRS], I32, name="pair_index_int")
+    nc.gpsimd.iota(pair_index_int[:], pattern=[[1, PAIRS]], base=0, channel_multiplier=0)
+    position_int = pool.tile([P, 1], I32, name="position_int")
+    for b in range(BATCH):
+        nc.gpsimd.iota(position_int[b * SEQ : (b + 1) * SEQ, :], pattern=[[0, 1]], base=0, channel_multiplier=1)
+    pair_index = pool.tile([P, PAIRS], F32, name="pair_index")
+    nc.vector.tensor_copy(out=pair_index[:], in_=pair_index_int[:])
+    position = pool.tile([P, 1], F32, name="position")
+    nc.vector.tensor_copy(out=position[:], in_=position_int[:])
+
+    frequency = pool.tile([P, PAIRS], F32, name="frequency")
+    nc.scalar.activation(out=frequency[:], in_=pair_index[:], func=ACT.Exp, scale=-math.log(ROPE_BASE) / PAIRS)
+    angle = pool.tile([P, PAIRS], F32, name="angle")
+    nc.vector.tensor_scalar_mul(out=angle[:], in0=frequency[:], scalar1=position[:, 0:1])
+
+    turns = pool.tile([P, PAIRS], F32, name="turns")
+    nc.vector.tensor_scalar(
+        out=turns[:], in0=angle[:], scalar1=1.0 / TWO_PI, scalar2=ROUND_MAGIC, op0=ALU.mult, op1=ALU.add
+    )
+    nc.vector.tensor_scalar_sub(out=turns[:], in0=turns[:], scalar1=ROUND_MAGIC)
+    reduced = pool.tile([P, PAIRS], F32, name="reduced")
+    nc.vector.scalar_tensor_tensor(
+        out=reduced[:], in0=turns[:], scalar=-TWO_PI_HIGH, in1=angle[:], op0=ALU.mult, op1=ALU.add
+    )
+    for part in (TWO_PI_MIDDLE, TWO_PI_LOW):
+        nc.vector.scalar_tensor_tensor(
+            out=reduced[:], in0=turns[:], scalar=-part, in1=reduced[:], op0=ALU.mult, op1=ALU.add
+        )
+
+    quarter_minus = pool.tile([P, PAIRS], F32, name="quarter_minus")
+    nc.vector.scalar_tensor_tensor(
+        out=quarter_minus[:], in0=reduced[:], scalar=-1.0, in1=reduced[:], op0=ALU.mult, op1=ALU.max
+    )
+    nc.vector.tensor_scalar(
+        out=quarter_minus[:], in0=quarter_minus[:], scalar1=-1.0, scalar2=math.pi / 2.0, op0=ALU.mult, op1=ALU.add
+    )
+
+    cos_pairs = pool.tile([P, PAIRS, 2], F32, name="cos_pairs")
+    nc.scalar.activation(
+        out=cos_pairs[:], in_=quarter_minus[:].unsqueeze(2).to_broadcast([P, PAIRS, 2]), func=ACT.Sin
+    )
+    sin_signed = pool.tile([P, 2, PAIRS], F32, name="sin_signed")
+    nc.scalar.activation(out=sin_signed[:, 0, :], in_=reduced[:], func=ACT.Sin, scale=-1.0)
+    nc.scalar.activation(out=sin_signed[:, 1, :], in_=reduced[:], func=ACT.Sin)
+    return cos_pairs, sin_signed
+
+
+def quantise_x(nc, pool, psum, x_sb, identity, x_codes, x_scales):
+    x_words = x_sb[:].bitcast(F32)
+    words_per_group = K_GROUP // 2
+    x_grouped = pool.tile([P, GROUPS, TOKENS, PACK], BF16, name="x_grouped", align_bytes=64)
+    x_grouped_words = x_grouped[:].bitcast(F32)
+
+    for bank in range(GROUPS // GROUPS_PER_BANK):
+        transposed = psum.tile([P, GROUPS_PER_BANK, 2, TOKENS], F32, name="transposed", tag="bank%d" % bank)
+        first = bank * GROUPS_PER_BANK
+        for j in range(GROUPS_PER_BANK):
+            start = (first + j) * words_per_group
+            for u in range(2):
+                nc.tensor.transpose(
+                    out=transposed[:, j, u, :],
+                    in_=x_words[:, start + u : start + words_per_group : 2],
+                    identity=identity[:],
+                )
+        copy = nc.vector.tensor_copy if bank % 2 == 0 else nc.scalar.copy
+        copy(
+            out=x_grouped_words[:, first : first + GROUPS_PER_BANK, :, :],
+            in_=transposed[:].rearrange("p g u t -> p g t u"),
+        )
+
+    for first in range(0, GROUPS, GROUPS_PER_BANK):
+        some = slice(first, first + GROUPS_PER_BANK)
+        nc.vector.quantize_mx(
+            out=x_codes[:, some, :].rearrange("p g t -> p (g t)").bitcast(FP8X4),
+            scales=x_scales[:, some, :].rearrange("p g t -> p (g t)"),
+            in_=x_grouped[:, some, :, :].rearrange("p g t k -> p (g t k)"),
+        )
+
+
+def tile_multiheadlatentattention_pb_k_kernel(tc, x, Wq_words, Wq_scales, out):
+    nc = tc.nc
+    x_rows = x.rearrange("b s k -> (b s) k")
+    out_rows = out.rearrange("b s h d -> (b s) (h d)")
+    dram_words = Wq_words.bitcast(I32)
+    dram_scales = Wq_scales.bitcast(I32)
+
+    with ExitStack() as ctx:
+        keep = ctx.enter_context(tc.tile_pool(name="keep", bufs=1))
+        w_ring = ctx.enter_context(tc.tile_pool(name="w_ring", bufs=W_BUFS))
+        work = ctx.enter_context(tc.tile_pool(name="work", bufs=2))
+        psum = ctx.enter_context(tc.psum_pool(name="psum", bufs=1))
+        ctx.enter_context(tc.manual_schedule())
+
+        x_sb = keep.tile([P, D_MODEL], BF16, name="x_sb")
+        x_cols = D_MODEL // X_LOADS
+        for i in range(X_LOADS):
+            cols = slice(i * x_cols, (i + 1) * x_cols)
+            nc.sync.dma_start(out=x_sb[:, cols], in_=x_rows[:, cols])
+        identity = keep.tile([P, P], F32, name="identity")
+        make_identity(nc, identity[:])
+
+        planes = keep.tile([P, GROUPS, N_OUT], U8, name="planes", align_bytes=64)
+        planes_int = planes[:].bitcast(I32)
+        for g in range(0, GROUPS, GROUPS_PER_SCALE_DMA):
+            nc.vector.memset(planes_int[:, g : g + GROUPS_PER_SCALE_DMA, :], 0)
+
+        def load_scales(first_group):
+            for g in range(first_group, first_group + STRETCH, GROUPS_PER_SCALE_DMA):
+                some = slice(g, g + GROUPS_PER_SCALE_DMA)
+                for half in range(2):
+                    for row in range(4):
+                        nc.sync.dma_start(
+                            out=planes_int[32 * half + row : P : 64, some, :],
+                            in_=dram_scales[some, 4 * half + row : SCALE_ROWS : 8, :].rearrange("g q n -> q g n"),
+                        )
+
+        w_tiles = {}
+        piece_ints = PIECE_BANKS * BANK_W_BYTES // 4
+
+        def fetch(t):
+            if t % STRETCH == 0:
+                load_scales(t)
+            w = w_ring.tile([P, GROUP_W_BYTES], U8, name="w", align_bytes=64)
+            if t < MAIN_GROUPS:
+                nc.sync.dma_start(out=w[:].bitcast(I32), in_=dram_words[t])
+            else:
+                piece = t - MAIN_GROUPS
+                nc.sync.dma_start(
+                    out=w[:].bitcast(I32).rearrange("p (g c) -> p g c", g=TAPER_GROUPS),
+                    in_=dram_words[MAIN_GROUPS:, :, piece * piece_ints : (piece + 1) * piece_ints].rearrange(
+                        "g p c -> p g c"
+                    ),
+                )
+            w_tiles[t] = w
+
+        for t in range(LOOKAHEAD):
+            fetch(t)
+
+        x_codes = keep.tile([P, GROUPS, TOKENS], U32, name="x_codes", align_bytes=64)
+        x_scales = keep.tile([P, GROUPS, TOKENS], U8, name="x_scales", align_bytes=64)
+        quantise_x(nc, keep, psum, x_sb, identity, x_codes, x_scales)
+        cos_pairs, sin_signed = build_rope_tables(nc, keep)
+
+        acc = [psum.tile([P, BANK_COLS], F32, name="acc%d" % bank, tag="bank%d" % bank) for bank in range(BANKS)]
+        out_sb = keep.tile([P, N_OUT], F32, name="out_sb")
+
+        def mx_pass(bank, g, w_cols):
+            nc.tensor.matmul_mx(
+                out=acc[bank][:],
+                lhsT=x_codes[:, g, :].bitcast(FP8X4),
+                lhsT_scale=x_scales[:, g, :],
+                rhs=w_cols.bitcast(FP4X4),
+                rhs_scale=planes[:, g, bank * BANK_COLS : (bank + 1) * BANK_COLS],
+                start=(g == 0),
+                stop=(g == GROUPS - 1),
+            )
+
+        def rope_and_store(bank):
+            cols = slice(bank * BANK_COLS, (bank + 1) * BANK_COLS)
+            q = acc[bank][:].rearrange("p (h d) -> p h d", h=HEADS_PER_BANK)
+            q_pairs = q[:, :, NOPE_DIM:].rearrange("p h (i e) -> p h i e", e=2)
+            result = out_sb[:, cols].rearrange("p (h d) -> p h d", h=HEADS_PER_BANK)
+            by_cos = work.tile([P, HEADS_PER_BANK, PAIRS, 2], F32, name="by_cos")
+            by_sin = work.tile([P, HEADS_PER_BANK, 2, PAIRS], F32, name="by_sin")
+            nc.vector.tensor_tensor(
+                out=by_cos[:],
+                in0=q_pairs,
+                in1=cos_pairs[:].unsqueeze(1).to_broadcast([P, HEADS_PER_BANK, PAIRS, 2]),
+                op=ALU.mult,
+            )
+            for e in range(2):
+                nc.vector.tensor_tensor(
+                    out=by_sin[:, :, e, :],
+                    in0=q_pairs[:, :, :, 1 - e],
+                    in1=sin_signed[:, e, :].unsqueeze(1).to_broadcast([P, HEADS_PER_BANK, PAIRS]),
+                    op=ALU.mult,
+                )
+            nc.scalar.copy(out=result[:, :, :NOPE_DIM], in_=q[:, :, :NOPE_DIM])
+            nc.vector.tensor_tensor(
+                out=result[:, :, NOPE_DIM:].rearrange("p h (i e) -> p h i e", e=2),
+                in0=by_cos[:],
+                in1=by_sin[:].rearrange("p h e i -> p h i e"),
+                op=ALU.add,
+            )
+            nc.sync.dma_start(out=out_rows[:, cols], in_=out_sb[:, cols])
+
+        for g in range(MAIN_GROUPS):
+            if g + LOOKAHEAD < W_TILES:
+                fetch(g + LOOKAHEAD)
+            for bank in range(BANKS):
+                mx_pass(bank, g, w_tiles[g][:, bank * BANK_W_BYTES : (bank + 1) * BANK_W_BYTES])
+
+        for piece in range(PIECES):
+            w = w_tiles[MAIN_GROUPS + piece][:].rearrange("p (g b) -> p g b", g=TAPER_GROUPS)
+            for j in range(PIECE_BANKS):
+                bank = piece * PIECE_BANKS + j
+                for i in range(TAPER_GROUPS):
+                    mx_pass(bank, MAIN_GROUPS + i, w[:, i, j * BANK_W_BYTES : (j + 1) * BANK_W_BYTES])
+                rope_and_store(bank)

@@ -39,8 +39,8 @@ GROUP_W_BYTES = N_OUT * 2
 X_LOADS = 4
 GROUPS_PER_BANK = 2
 
-STRETCH = 16
-GROUPS_PER_SCALE_DMA = 4
+WORDS_FIRST = 6
+SCALE_CHUNKS = [(0, 4), (4, 12), (12, 14), (14, 16)]
 
 TAPER_GROUPS = 4
 PIECE_BANKS = 2
@@ -48,9 +48,8 @@ MAIN_GROUPS = GROUPS - TAPER_GROUPS
 PIECES = BANKS // PIECE_BANKS
 W_TILES = MAIN_GROUPS + PIECES
 assert TAPER_GROUPS * PIECE_BANKS * BANK_W_BYTES == GROUP_W_BYTES
-assert STRETCH % TAPER_GROUPS == 0
 
-W_BUFS = 8
+W_BUFS = 12
 LOOKAHEAD = W_BUFS - 1
 assert LOOKAHEAD >= PIECES
 
@@ -165,27 +164,33 @@ def tile_multiheadlatentattention_pb_k_kernel(tc, x, Wq_words, Wq_scales, out):
         identity = keep.tile([P, P], F32, name="identity")
         make_identity(nc, identity[:])
 
-        planes = keep.tile([P, GROUPS, N_OUT], U8, name="planes", align_bytes=64)
-        planes_int = planes[:].bitcast(I32)
-        for g in range(0, GROUPS, GROUPS_PER_SCALE_DMA):
-            nc.vector.memset(planes_int[:, g : g + GROUPS_PER_SCALE_DMA, :], 0)
+        planes = []
+        for first, last in SCALE_CHUNKS:
+            tile = keep.tile([P, last - first, N_OUT], U8, name="planes%d" % first, align_bytes=64)
+            planes.append(tile)
+            nc.vector.memset(tile[:].bitcast(I32), 0)
 
-        def load_scales(first_group):
-            for g in range(first_group, first_group + STRETCH, GROUPS_PER_SCALE_DMA):
-                some = slice(g, g + GROUPS_PER_SCALE_DMA)
+        def load_scales():
+            for tile, (first, last) in zip(planes, SCALE_CHUNKS):
                 for half in range(2):
                     for row in range(4):
                         nc.sync.dma_start(
-                            out=planes_int[32 * half + row : P : 64, some, :],
-                            in_=dram_scales[some, 4 * half + row : SCALE_ROWS : 8, :].rearrange("g q n -> q g n"),
+                            out=tile[:].bitcast(I32)[32 * half + row : P : 64, :, :],
+                            in_=dram_scales[first:last, 4 * half + row : SCALE_ROWS : 8, :].rearrange("g q n -> q g n"),
                         )
+
+        def plane(g, bank):
+            for tile, (first, last) in zip(planes, SCALE_CHUNKS):
+                if first <= g < last:
+                    found = tile[:, g - first, bank * BANK_COLS : (bank + 1) * BANK_COLS]
+            return found
 
         w_tiles = {}
         piece_ints = PIECE_BANKS * BANK_W_BYTES // 4
 
         def fetch(t):
-            if t % STRETCH == 0:
-                load_scales(t)
+            if t == WORDS_FIRST:
+                load_scales()
             w = w_ring.tile([P, GROUP_W_BYTES], U8, name="w", align_bytes=64)
             if t < MAIN_GROUPS:
                 nc.sync.dma_start(out=w[:].bitcast(I32), in_=dram_words[t])
@@ -216,7 +221,7 @@ def tile_multiheadlatentattention_pb_k_kernel(tc, x, Wq_words, Wq_scales, out):
                 lhsT=x_codes[:, g, :].bitcast(FP8X4),
                 lhsT_scale=x_scales[:, g, :],
                 rhs=w_cols.bitcast(FP4X4),
-                rhs_scale=planes[:, g, bank * BANK_COLS : (bank + 1) * BANK_COLS],
+                rhs_scale=plane(g, bank),
                 start=(g == 0),
                 stop=(g == GROUPS - 1),
             )

@@ -36,7 +36,7 @@ HEADS_PER_BANK = BANK_COLS // HEAD_DIM
 BANK_W_BYTES = BANK_COLS * 2
 GROUP_W_BYTES = N_OUT * 2
 
-X_LOADS = 4
+X_LOADS = 1
 GROUPS_PER_BANK = 2
 
 WORDS_FIRST = 6
@@ -44,14 +44,18 @@ SCALE_CHUNKS = [(0, 4), (4, 12), (12, 14), (14, 16)]
 
 TAPER_GROUPS = 4
 PIECE_BANKS = 2
+PART_GROUPS = 2
+HALF_BANKS = BANKS // 2
+HALF_W_BYTES = HALF_BANKS * BANK_W_BYTES
 MAIN_GROUPS = GROUPS - TAPER_GROUPS
-PIECES = BANKS // PIECE_BANKS
-W_TILES = MAIN_GROUPS + PIECES
-assert TAPER_GROUPS * PIECE_BANKS * BANK_W_BYTES == GROUP_W_BYTES
+HALVES = [(g, h) for g in range(WORDS_FIRST, MAIN_GROUPS) for h in range(2)]
+PARTS = [(bank, g) for bank in range(0, BANKS, PIECE_BANKS) for g in range(MAIN_GROUPS, GROUPS, PART_GROUPS)]
+assert PART_GROUPS * PIECE_BANKS == HALF_BANKS
+SMALL_TILES = len(HALVES) + len(PARTS)
 
-W_BUFS = 12
-LOOKAHEAD = W_BUFS - 1
-assert LOOKAHEAD >= PIECES
+SMALL_BUFS = 12
+LOOKAHEAD = SMALL_BUFS - 1
+assert LOOKAHEAD >= len(PARTS)
 
 TWO_PI = 2.0 * math.pi
 TWO_PI_HIGH = 6.28125
@@ -151,8 +155,8 @@ def tile_multiheadlatentattention_pb_k_kernel(tc, x, Wq_words, Wq_scales, out):
 
     with ExitStack() as ctx:
         keep = ctx.enter_context(tc.tile_pool(name="keep", bufs=1))
-        w_ring = ctx.enter_context(tc.tile_pool(name="w_ring", bufs=W_BUFS))
-        work = ctx.enter_context(tc.tile_pool(name="work", bufs=2))
+        w_ring = ctx.enter_context(tc.tile_pool(name="w_ring", bufs=SMALL_BUFS))
+        work = ctx.enter_context(tc.tile_pool(name="work", bufs=3))
         psum = ctx.enter_context(tc.psum_pool(name="psum", bufs=1))
         ctx.enter_context(tc.manual_schedule())
 
@@ -185,27 +189,35 @@ def tile_multiheadlatentattention_pb_k_kernel(tc, x, Wq_words, Wq_scales, out):
                     found = tile[:, g - first, bank * BANK_COLS : (bank + 1) * BANK_COLS]
             return found
 
-        w_tiles = {}
-        piece_ints = PIECE_BANKS * BANK_W_BYTES // 4
+        first_w = []
+        for g in range(WORDS_FIRST):
+            w = keep.tile([P, GROUP_W_BYTES], U8, name="first_w%d" % g, align_bytes=64)
+            nc.sync.dma_start(out=w[:].bitcast(I32), in_=dram_words[g])
+            first_w.append(w)
+        load_scales()
 
-        def fetch(t):
-            if t == WORDS_FIRST:
-                load_scales()
-            w = w_ring.tile([P, GROUP_W_BYTES], U8, name="w", align_bytes=64)
-            if t < MAIN_GROUPS:
-                nc.sync.dma_start(out=w[:].bitcast(I32), in_=dram_words[t])
+        small_tiles = []
+
+        def fetch_small():
+            t = len(small_tiles)
+            w = w_ring.tile([P, HALF_W_BYTES], U8, name="w", align_bytes=64)
+            if t < len(HALVES):
+                g, half = HALVES[t]
+                ints = HALF_W_BYTES // 4
+                nc.sync.dma_start(out=w[:].bitcast(I32), in_=dram_words[g, :, half * ints : (half + 1) * ints])
             else:
-                piece = t - MAIN_GROUPS
+                bank, g = PARTS[t - len(HALVES)]
+                ints = BANK_W_BYTES // 4
                 nc.sync.dma_start(
-                    out=w[:].bitcast(I32).rearrange("p (g c) -> p g c", g=TAPER_GROUPS),
-                    in_=dram_words[MAIN_GROUPS:, :, piece * piece_ints : (piece + 1) * piece_ints].rearrange(
+                    out=w[:].bitcast(I32).rearrange("p (g c) -> p g c", g=PART_GROUPS),
+                    in_=dram_words[g : g + PART_GROUPS, :, bank * ints : (bank + PIECE_BANKS) * ints].rearrange(
                         "g p c -> p g c"
                     ),
                 )
-            w_tiles[t] = w
+            small_tiles.append(w)
 
         for t in range(LOOKAHEAD):
-            fetch(t)
+            fetch_small()
 
         x_codes = keep.tile([P, GROUPS, TOKENS], U32, name="x_codes", align_bytes=64)
         x_scales = keep.tile([P, GROUPS, TOKENS], U8, name="x_scales", align_bytes=64)
@@ -247,7 +259,8 @@ def tile_multiheadlatentattention_pb_k_kernel(tc, x, Wq_words, Wq_scales, out):
                     op=ALU.mult,
                 )
             nc.scalar.copy(out=result[:, :, :NOPE_DIM], in_=q[:, :, :NOPE_DIM])
-            nc.vector.tensor_tensor(
+            adder = nc.vector if bank == BANKS - 1 else nc.gpsimd
+            adder.tensor_tensor(
                 out=result[:, :, NOPE_DIM:].rearrange("p h (i e) -> p h i e", e=2),
                 in0=by_cos[:],
                 in1=by_sin[:].rearrange("p h e i -> p h i e"),
@@ -255,16 +268,23 @@ def tile_multiheadlatentattention_pb_k_kernel(tc, x, Wq_words, Wq_scales, out):
             )
             nc.sync.dma_start(out=out_rows[:, cols], in_=out_sb[:, cols])
 
-        for g in range(MAIN_GROUPS):
-            if g + LOOKAHEAD < W_TILES:
-                fetch(g + LOOKAHEAD)
+        for g in range(WORDS_FIRST):
             for bank in range(BANKS):
-                mx_pass(bank, g, w_tiles[g][:, bank * BANK_W_BYTES : (bank + 1) * BANK_W_BYTES])
+                mx_pass(bank, g, first_w[g][:, bank * BANK_W_BYTES : (bank + 1) * BANK_W_BYTES])
 
-        for piece in range(PIECES):
-            w = w_tiles[MAIN_GROUPS + piece][:].rearrange("p (g b) -> p g b", g=TAPER_GROUPS)
-            for j in range(PIECE_BANKS):
-                bank = piece * PIECE_BANKS + j
-                for i in range(TAPER_GROUPS):
-                    mx_pass(bank, MAIN_GROUPS + i, w[:, i, j * BANK_W_BYTES : (j + 1) * BANK_W_BYTES])
-                rope_and_store(bank)
+        for t in range(SMALL_TILES):
+            if len(small_tiles) < SMALL_TILES:
+                fetch_small()
+            w = small_tiles[t]
+            if t < len(HALVES):
+                g, half = HALVES[t]
+                for j in range(HALF_BANKS):
+                    mx_pass(half * HALF_BANKS + j, g, w[:, j * BANK_W_BYTES : (j + 1) * BANK_W_BYTES])
+            else:
+                first_bank, first_group = PARTS[t - len(HALVES)]
+                for j in range(PIECE_BANKS):
+                    for i in range(PART_GROUPS):
+                        start = (i * PIECE_BANKS + j) * BANK_W_BYTES
+                        mx_pass(first_bank + j, first_group + i, w[:, start : start + BANK_W_BYTES])
+                    if first_group + PART_GROUPS == GROUPS:
+                        rope_and_store(first_bank + j)

@@ -43,19 +43,18 @@ WORDS_FIRST = 6
 SCALE_CHUNKS = [(0, 4), (4, 12), (12, 14), (14, 16)]
 
 TAPER_GROUPS = 4
-PIECE_BANKS = 2
-PART_GROUPS = 2
-HALF_BANKS = BANKS // 2
-HALF_W_BYTES = HALF_BANKS * BANK_W_BYTES
 MAIN_GROUPS = GROUPS - TAPER_GROUPS
-HALVES = [(g, h) for g in range(WORDS_FIRST, MAIN_GROUPS) for h in range(2)]
-PARTS = [(bank, g) for bank in range(0, BANKS, PIECE_BANKS) for g in range(MAIN_GROUPS, GROUPS, PART_GROUPS)]
-assert PART_GROUPS * PIECE_BANKS == HALF_BANKS
-SMALL_TILES = len(HALVES) + len(PARTS)
+HALF_BANKS = BANKS // 2
+HALF_GROUPS = [(b, b + HALF_BANKS, g, g + 1) for g in range(WORDS_FIRST, MAIN_GROUPS) for b in (0, HALF_BANKS)]
+TAPER_RANGES = [(0, 4, 1), (4, 6, 2), (6, 7, 2), (7, 8, 2)]
+TAPER = [(b, e, g, g + n) for b, e, n in TAPER_RANGES for g in range(MAIN_GROUPS, GROUPS, n)]
+TILES = HALF_GROUPS + TAPER
+TILE_W_BYTES = HALF_BANKS * BANK_W_BYTES
+STORES = [(0, 2), (2, 4), (4, 6), (6, 7), (7, 8)]
 
-SMALL_BUFS = 12
-LOOKAHEAD = SMALL_BUFS - 1
-assert LOOKAHEAD >= len(PARTS)
+TILE_BUFS = 12
+LOOKAHEAD = TILE_BUFS - 1
+assert LOOKAHEAD >= len(TAPER) - TAPER_GROUPS
 
 TWO_PI = 2.0 * math.pi
 TWO_PI_HIGH = 6.28125
@@ -108,10 +107,10 @@ def build_rope_tables(nc, pool):
     nc.scalar.activation(
         out=cos_pairs[:], in_=quarter_minus[:].unsqueeze(2).to_broadcast([P, PAIRS, 2]), func=ACT.Sin
     )
-    sin_signed = pool.tile([P, 2, PAIRS], F32, name="sin_signed")
-    nc.scalar.activation(out=sin_signed[:, 0, :], in_=reduced[:], func=ACT.Sin, scale=-1.0)
-    nc.scalar.activation(out=sin_signed[:, 1, :], in_=reduced[:], func=ACT.Sin)
-    return cos_pairs, sin_signed
+    sin_pairs = pool.tile([P, PAIRS, 2], F32, name="sin_pairs")
+    nc.scalar.activation(out=sin_pairs[:, :, 0], in_=reduced[:], func=ACT.Sin, scale=-1.0)
+    nc.scalar.activation(out=sin_pairs[:, :, 1], in_=reduced[:], func=ACT.Sin)
+    return cos_pairs, sin_pairs
 
 
 def quantise_x(nc, pool, psum, x_sb, identity, x_codes, x_scales):
@@ -155,7 +154,7 @@ def tile_multiheadlatentattention_pb_k_kernel(tc, x, Wq_words, Wq_scales, out):
 
     with ExitStack() as ctx:
         keep = ctx.enter_context(tc.tile_pool(name="keep", bufs=1))
-        w_ring = ctx.enter_context(tc.tile_pool(name="w_ring", bufs=SMALL_BUFS))
+        w_ring = ctx.enter_context(tc.tile_pool(name="w_ring", bufs=TILE_BUFS))
         work = ctx.enter_context(tc.tile_pool(name="work", bufs=3))
         psum = ctx.enter_context(tc.psum_pool(name="psum", bufs=1))
         ctx.enter_context(tc.manual_schedule())
@@ -196,33 +195,26 @@ def tile_multiheadlatentattention_pb_k_kernel(tc, x, Wq_words, Wq_scales, out):
             first_w.append(w)
         load_scales()
 
-        small_tiles = []
+        tiles = []
 
-        def fetch_small():
-            t = len(small_tiles)
-            w = w_ring.tile([P, HALF_W_BYTES], U8, name="w", align_bytes=64)
-            if t < len(HALVES):
-                g, half = HALVES[t]
-                ints = HALF_W_BYTES // 4
-                nc.sync.dma_start(out=w[:].bitcast(I32), in_=dram_words[g, :, half * ints : (half + 1) * ints])
-            else:
-                bank, g = PARTS[t - len(HALVES)]
-                ints = BANK_W_BYTES // 4
-                nc.sync.dma_start(
-                    out=w[:].bitcast(I32).rearrange("p (g c) -> p g c", g=PART_GROUPS),
-                    in_=dram_words[g : g + PART_GROUPS, :, bank * ints : (bank + PIECE_BANKS) * ints].rearrange(
-                        "g p c -> p g c"
-                    ),
-                )
-            small_tiles.append(w)
+        def fetch_tile():
+            bank, bank_end, g, g_end = TILES[len(tiles)]
+            w = w_ring.tile([P, TILE_W_BYTES], U8, name="w", align_bytes=64)
+            row_bytes = (bank_end - bank) * BANK_W_BYTES
+            ints = BANK_W_BYTES // 4
+            nc.sync.dma_start(
+                out=w[:, : (g_end - g) * row_bytes].bitcast(I32).rearrange("p (g c) -> p g c", g=g_end - g),
+                in_=dram_words[g:g_end, :, bank * ints : bank_end * ints].rearrange("g p c -> p g c"),
+            )
+            tiles.append(w)
 
         for t in range(LOOKAHEAD):
-            fetch_small()
+            fetch_tile()
 
         x_codes = keep.tile([P, GROUPS, TOKENS], U32, name="x_codes", align_bytes=64)
         x_scales = keep.tile([P, GROUPS, TOKENS], U8, name="x_scales", align_bytes=64)
         quantise_x(nc, keep, psum, x_sb, identity, x_codes, x_scales)
-        cos_pairs, sin_signed = build_rope_tables(nc, keep)
+        cos_pairs, sin_pairs = build_rope_tables(nc, keep)
 
         acc = [psum.tile([P, BANK_COLS], F32, name="acc%d" % bank, tag="bank%d" % bank) for bank in range(BANKS)]
         out_sb = keep.tile([P, N_OUT], F32, name="out_sb")
@@ -238,24 +230,18 @@ def tile_multiheadlatentattention_pb_k_kernel(tc, x, Wq_words, Wq_scales, out):
                 stop=(g == GROUPS - 1),
             )
 
-        def rope_and_store(bank):
+        def rope(bank):
             cols = slice(bank * BANK_COLS, (bank + 1) * BANK_COLS)
             q = acc[bank][:].rearrange("p (h d) -> p h d", h=HEADS_PER_BANK)
             q_pairs = q[:, :, NOPE_DIM:].rearrange("p h (i e) -> p h i e", e=2)
             result = out_sb[:, cols].rearrange("p (h d) -> p h d", h=HEADS_PER_BANK)
             by_cos = work.tile([P, HEADS_PER_BANK, PAIRS, 2], F32, name="by_cos")
-            by_sin = work.tile([P, HEADS_PER_BANK, 2, PAIRS], F32, name="by_sin")
-            nc.vector.tensor_tensor(
-                out=by_cos[:],
-                in0=q_pairs,
-                in1=cos_pairs[:].unsqueeze(1).to_broadcast([P, HEADS_PER_BANK, PAIRS, 2]),
-                op=ALU.mult,
-            )
-            for e in range(2):
+            by_sin = work.tile([P, HEADS_PER_BANK, PAIRS, 2], F32, name="by_sin")
+            for product, pairs, table in ((by_cos, q_pairs, cos_pairs), (by_sin, q_pairs[:, :, :, ::-1], sin_pairs)):
                 nc.vector.tensor_tensor(
-                    out=by_sin[:, :, e, :],
-                    in0=q_pairs[:, :, :, 1 - e],
-                    in1=sin_signed[:, e, :].unsqueeze(1).to_broadcast([P, HEADS_PER_BANK, PAIRS]),
+                    out=product[:],
+                    in0=pairs,
+                    in1=table[:].unsqueeze(1).to_broadcast([P, HEADS_PER_BANK, PAIRS, 2]),
                     op=ALU.mult,
                 )
             nc.scalar.copy(out=result[:, :, :NOPE_DIM], in_=q[:, :, :NOPE_DIM])
@@ -263,28 +249,28 @@ def tile_multiheadlatentattention_pb_k_kernel(tc, x, Wq_words, Wq_scales, out):
             adder.tensor_tensor(
                 out=result[:, :, NOPE_DIM:].rearrange("p h (i e) -> p h i e", e=2),
                 in0=by_cos[:],
-                in1=by_sin[:].rearrange("p h e i -> p h i e"),
+                in1=by_sin[:],
                 op=ALU.add,
             )
-            nc.sync.dma_start(out=out_rows[:, cols], in_=out_sb[:, cols])
 
         for g in range(WORDS_FIRST):
             for bank in range(BANKS):
                 mx_pass(bank, g, first_w[g][:, bank * BANK_W_BYTES : (bank + 1) * BANK_W_BYTES])
 
-        for t in range(SMALL_TILES):
-            if len(small_tiles) < SMALL_TILES:
-                fetch_small()
-            w = small_tiles[t]
-            if t < len(HALVES):
-                g, half = HALVES[t]
-                for j in range(HALF_BANKS):
-                    mx_pass(half * HALF_BANKS + j, g, w[:, j * BANK_W_BYTES : (j + 1) * BANK_W_BYTES])
-            else:
-                first_bank, first_group = PARTS[t - len(HALVES)]
-                for j in range(PIECE_BANKS):
-                    for i in range(PART_GROUPS):
-                        start = (i * PIECE_BANKS + j) * BANK_W_BYTES
-                        mx_pass(first_bank + j, first_group + i, w[:, start : start + BANK_W_BYTES])
-                    if first_group + PART_GROUPS == GROUPS:
-                        rope_and_store(first_bank + j)
+        finished = 0
+        for t in range(len(TILES)):
+            if len(tiles) < len(TILES):
+                fetch_tile()
+            first_bank, bank_end, first_group, group_end = TILES[t]
+            row_bytes = (bank_end - first_bank) * BANK_W_BYTES
+            for bank in range(first_bank, bank_end):
+                for g in range(first_group, group_end):
+                    start = (g - first_group) * row_bytes + (bank - first_bank) * BANK_W_BYTES
+                    mx_pass(bank, g, tiles[t][:, start : start + BANK_W_BYTES])
+                if group_end == GROUPS:
+                    rope(bank)
+                    finished = finished + 1
+                    for store_bank, store_end in STORES:
+                        if store_end == finished:
+                            cols = slice(store_bank * BANK_COLS, store_end * BANK_COLS)
+                            nc.sync.dma_start(out=out_rows[:, cols], in_=out_sb[:, cols])

@@ -178,7 +178,7 @@ def tile_multiheadlatentattention_pb_k_kernel(tc, x, Wq_words, Wq_scales, out):
                 for half in range(2):
                     for row in range(4):
                         nc.sync.dma_start(
-                            out=tile[:].bitcast(I32)[32 * half + row : P : 64, :, :],
+                            out=tile[:].bitcast(I32).rearrange("p g n -> p (g n)")[32 * half + row : P : 64, :],
                             in_=dram_scales[first:last, 4 * half + row : SCALE_ROWS : 8, :].rearrange("g q n -> q g n"),
                         )
 

@@ -40,7 +40,7 @@ X_LOADS = 1
 GROUPS_PER_BANK = 2
 
 WORDS_FIRST = 6
-SCALE_CHUNKS = [(0, 4), (4, 12), (12, 14), (14, 16)]
+SCALE_CHUNKS = [(0, 4), (4, 10), (10, 16)]
 
 TAPER_GROUPS = 4
 MAIN_GROUPS = GROUPS - TAPER_GROUPS
@@ -199,7 +199,7 @@ def tile_multiheadlatentattention_pb_k_kernel(tc, x, Wq_words, Wq_scales, out):
 
         def fetch_tile():
             bank, bank_end, g, g_end = TILES[len(tiles)]
-            w = w_ring.tile([P, TILE_W_BYTES], U8, name="w", align_bytes=64)
+            w = w_ring.tile([P, TILE_W_BYTES], U8, name="w", align_bytes=64) if tiles else gate_tile
             row_bytes = (bank_end - bank) * BANK_W_BYTES
             ints = BANK_W_BYTES // 4
             nc.sync.dma_start(
@@ -208,13 +208,18 @@ def tile_multiheadlatentattention_pb_k_kernel(tc, x, Wq_words, Wq_scales, out):
             )
             tiles.append(w)
 
-        for t in range(LOOKAHEAD):
-            fetch_tile()
-
         x_codes = keep.tile([P, GROUPS, TOKENS], U32, name="x_codes", align_bytes=64)
         x_scales = keep.tile([P, GROUPS, TOKENS], U8, name="x_scales", align_bytes=64)
         quantise_x(nc, keep, psum, x_sb, identity, x_codes, x_scales)
         cos_pairs, sin_pairs = build_rope_tables(nc, keep)
+
+        gate_rows = slice(32, 32 + 2)
+        gate_tile = w_ring.tile([P, TILE_W_BYTES], U8, name="w", align_bytes=64)
+        nc.vector.tensor_copy(
+            out=gate_tile[gate_rows, 0:4].bitcast(I32), in_=planes[len(planes) - 1][gate_rows, 0, 0:4].bitcast(I32)
+        )
+        for t in range(LOOKAHEAD):
+            fetch_tile()
 
         acc = [psum.tile([P, BANK_COLS], F32, name="acc%d" % bank, tag="bank%d" % bank) for bank in range(BANKS)]
         out_sb = keep.tile([P, N_OUT], F32, name="out_sb")

@@ -40,7 +40,7 @@ X_LOADS = 1
 GROUPS_PER_BANK = 2
 
 WORDS_FIRST = 6
-SCALE_CHUNKS = [(0, 4), (4, 10), (10, 16)]
+SCALE_CHUNKS = [(0, 4), (4, 9), (9, 16)]
 
 TAPER_GROUPS = 4
 MAIN_GROUPS = GROUPS - TAPER_GROUPS

import math
from contextlib import ExitStack

import concourse.mybir as mybir
from concourse.masks import make_identity

F32 = mybir.dt.float32
BF16 = mybir.dt.bfloat16
I32 = mybir.dt.int32
U32 = mybir.dt.uint32
U8 = mybir.dt.uint8
FP8X4 = mybir.dt.float8_e4m3fn_x4
FP4X4 = mybir.dt.float4_e2m1fn_x4
ALU = mybir.AluOpType
ACT = mybir.ActivationFunctionType

P = 128
BATCH = 2
SEQ = 64
TOKENS = BATCH * SEQ
D_MODEL = 8192
HEADS = 16
HEAD_DIM = 256
NOPE_DIM = 128
N_OUT = HEADS * HEAD_DIM
PAIRS = (HEAD_DIM - NOPE_DIM) // 2
ROPE_BASE = 10000.0

PACK = 4
K_GROUP = P * PACK
GROUPS = D_MODEL // K_GROUP
SCALE_ROWS = K_GROUP // 32
BANK_COLS = 512
BANKS = N_OUT // BANK_COLS
HEADS_PER_BANK = BANK_COLS // HEAD_DIM
BANK_W_BYTES = BANK_COLS * 2
GROUP_W_BYTES = N_OUT * 2

X_LOADS = 1
GROUPS_PER_BANK = 2

WORDS_FIRST = 6
SCALE_CHUNKS = [(0, 4), (4, 9), (9, 16)]

TAPER_GROUPS = 4
MAIN_GROUPS = GROUPS - TAPER_GROUPS
HALF_BANKS = BANKS // 2
HALF_GROUPS = [(b, b + HALF_BANKS, g, g + 1) for g in range(WORDS_FIRST, MAIN_GROUPS) for b in (0, HALF_BANKS)]
TAPER_RANGES = [(0, 4, 1), (4, 6, 2), (6, 7, 2), (7, 8, 2)]
TAPER = [(b, e, g, g + n) for b, e, n in TAPER_RANGES for g in range(MAIN_GROUPS, GROUPS, n)]
TILES = HALF_GROUPS + TAPER
TILE_W_BYTES = HALF_BANKS * BANK_W_BYTES
STORES = [(0, 2), (2, 4), (4, 6), (6, 7), (7, 8)]

TILE_BUFS = 12
LOOKAHEAD = TILE_BUFS - 1
assert LOOKAHEAD >= len(TAPER) - TAPER_GROUPS

TWO_PI = 2.0 * math.pi
TWO_PI_HIGH = 6.28125
TWO_PI_MIDDLE = math.floor((TWO_PI - TWO_PI_HIGH) * 2.0**21) / 2.0**21
TWO_PI_LOW = TWO_PI - TWO_PI_HIGH - TWO_PI_MIDDLE
ROUND_MAGIC = 1.5 * 2.0**23

FLOPS = 2 * TOKENS * D_MODEL * N_OUT


def build_rope_tables(nc, pool):
    pair_index_int = pool.tile([P, PAIRS], I32, name="pair_index_int")
    nc.gpsimd.iota(pair_index_int[:], pattern=[[1, PAIRS]], base=0, channel_multiplier=0)
    position_int = pool.tile([P, 1], I32, name="position_int")
    for b in range(BATCH):
        nc.gpsimd.iota(position_int[b * SEQ : (b + 1) * SEQ, :], pattern=[[0, 1]], base=0, channel_multiplier=1)
    pair_index = pool.tile([P, PAIRS], F32, name="pair_index")
    nc.vector.tensor_copy(out=pair_index[:], in_=pair_index_int[:])
    position = pool.tile([P, 1], F32, name="position")
    nc.vector.tensor_copy(out=position[:], in_=position_int[:])

    frequency = pool.tile([P, PAIRS], F32, name="frequency")
    nc.scalar.activation(out=frequency[:], in_=pair_index[:], func=ACT.Exp, scale=-math.log(ROPE_BASE) / PAIRS)
    angle = pool.tile([P, PAIRS], F32, name="angle")
    nc.vector.tensor_scalar_mul(out=angle[:], in0=frequency[:], scalar1=position[:, 0:1])

    turns = pool.tile([P, PAIRS], F32, name="turns")
    nc.vector.tensor_scalar(
        out=turns[:], in0=angle[:], scalar1=1.0 / TWO_PI, scalar2=ROUND_MAGIC, op0=ALU.mult, op1=ALU.add
    )
    nc.vector.tensor_scalar_sub(out=turns[:], in0=turns[:], scalar1=ROUND_MAGIC)
    reduced = pool.tile([P, PAIRS], F32, name="reduced")
    nc.vector.scalar_tensor_tensor(
        out=reduced[:], in0=turns[:], scalar=-TWO_PI_HIGH, in1=angle[:], op0=ALU.mult, op1=ALU.add
    )
    for part in (TWO_PI_MIDDLE, TWO_PI_LOW):
        nc.vector.scalar_tensor_tensor(
            out=reduced[:], in0=turns[:], scalar=-part, in1=reduced[:], op0=ALU.mult, op1=ALU.add
        )

    quarter_minus = pool.tile([P, PAIRS], F32, name="quarter_minus")
    nc.vector.scalar_tensor_tensor(
        out=quarter_minus[:], in0=reduced[:], scalar=-1.0, in1=reduced[:], op0=ALU.mult, op1=ALU.max
    )
    nc.vector.tensor_scalar(
        out=quarter_minus[:], in0=quarter_minus[:], scalar1=-1.0, scalar2=math.pi / 2.0, op0=ALU.mult, op1=ALU.add
    )

    cos_pairs = pool.tile([P, PAIRS, 2], F32, name="cos_pairs")
    nc.scalar.activation(
        out=cos_pairs[:], in_=quarter_minus[:].unsqueeze(2).to_broadcast([P, PAIRS, 2]), func=ACT.Sin
    )
    sin_pairs = pool.tile([P, PAIRS, 2], F32, name="sin_pairs")
    nc.scalar.activation(out=sin_pairs[:, :, 0], in_=reduced[:], func=ACT.Sin, scale=-1.0)
    nc.scalar.activation(out=sin_pairs[:, :, 1], in_=reduced[:], func=ACT.Sin)
    return cos_pairs, sin_pairs


def quantise_x(nc, pool, psum, x_sb, identity, x_codes, x_scales):
    x_words = x_sb[:].bitcast(F32)
    words_per_group = K_GROUP // 2
    x_grouped = pool.tile([P, GROUPS, TOKENS, PACK], BF16, name="x_grouped", align_bytes=64)
    x_grouped_words = x_grouped[:].bitcast(F32)

    for bank in range(GROUPS // GROUPS_PER_BANK):
        transposed = psum.tile([P, GROUPS_PER_BANK, 2, TOKENS], F32, name="transposed", tag="bank%d" % bank)
        first = bank * GROUPS_PER_BANK
        for j in range(GROUPS_PER_BANK):
            start = (first + j) * words_per_group
            for u in range(2):
                nc.tensor.transpose(
                    out=transposed[:, j, u, :],
                    in_=x_words[:, start + u : start + words_per_group : 2],
                    identity=identity[:],
                )
        copy = nc.vector.tensor_copy if bank % 2 == 0 else nc.scalar.copy
        copy(
            out=x_grouped_words[:, first : first + GROUPS_PER_BANK, :, :],
            in_=transposed[:].rearrange("p g u t -> p g t u"),
        )

    for first in range(0, GROUPS, GROUPS_PER_BANK):
        some = slice(first, first + GROUPS_PER_BANK)
        nc.vector.quantize_mx(
            out=x_codes[:, some, :].rearrange("p g t -> p (g t)").bitcast(FP8X4),
            scales=x_scales[:, some, :].rearrange("p g t -> p (g t)"),
            in_=x_grouped[:, some, :, :].rearrange("p g t k -> p (g t k)"),
        )


def tile_multiheadlatentattention_pb_k_kernel(tc, x, Wq_words, Wq_scales, out):
    nc = tc.nc
    x_rows = x.rearrange("b s k -> (b s) k")
    out_rows = out.rearrange("b s h d -> (b s) (h d)")
    dram_words = Wq_words.bitcast(I32)
    dram_scales = Wq_scales.bitcast(I32)

    with ExitStack() as ctx:
        keep = ctx.enter_context(tc.tile_pool(name="keep", bufs=1))
        w_ring = ctx.enter_context(tc.tile_pool(name="w_ring", bufs=TILE_BUFS))
        work = ctx.enter_context(tc.tile_pool(name="work", bufs=3))
        psum = ctx.enter_context(tc.psum_pool(name="psum", bufs=1))
        ctx.enter_context(tc.manual_schedule())

        x_sb = keep.tile([P, D_MODEL], BF16, name="x_sb")
        x_cols = D_MODEL // X_LOADS
        for i in range(X_LOADS):
            cols = slice(i * x_cols, (i + 1) * x_cols)
            nc.sync.dma_start(out=x_sb[:, cols], in_=x_rows[:, cols])
        identity = keep.tile([P, P], F32, name="identity")
        make_identity(nc, identity[:])

        planes = []
        for first, last in SCALE_CHUNKS:
            tile = keep.tile([P, last - first, N_OUT], U8, name="planes%d" % first, align_bytes=64)
            planes.append(tile)
            nc.vector.memset(tile[:].bitcast(I32), 0)

        def load_scales():
            for tile, (first, last) in zip(planes, SCALE_CHUNKS):
                for half in range(2):
                    for row in range(4):
                        nc.sync.dma_start(
                            out=tile[:].bitcast(I32).rearrange("p g n -> p (g n)")[32 * half + row : P : 64, :],
                            in_=dram_scales[first:last, 4 * half + row : SCALE_ROWS : 8, :].rearrange("g q n -> q g n"),
                        )

        def plane(g, bank):
            for tile, (first, last) in zip(planes, SCALE_CHUNKS):
                if first <= g < last:
                    found = tile[:, g - first, bank * BANK_COLS : (bank + 1) * BANK_COLS]
            return found

        first_w = []
        for g in range(WORDS_FIRST):
            w = keep.tile([P, GROUP_W_BYTES], U8, name="first_w%d" % g, align_bytes=64)
            nc.sync.dma_start(out=w[:].bitcast(I32), in_=dram_words[g])
            first_w.append(w)
        load_scales()

        tiles = []

        def fetch_tile():
            bank, bank_end, g, g_end = TILES[len(tiles)]
            w = w_ring.tile([P, TILE_W_BYTES], U8, name="w", align_bytes=64) if tiles else gate_tile
            row_bytes = (bank_end - bank) * BANK_W_BYTES
            ints = BANK_W_BYTES // 4
            nc.sync.dma_start(
                out=w[:, : (g_end - g) * row_bytes].bitcast(I32).rearrange("p (g c) -> p g c", g=g_end - g),
                in_=dram_words[g:g_end, :, bank * ints : bank_end * ints].rearrange("g p c -> p g c"),
            )
            tiles.append(w)

        x_codes = keep.tile([P, GROUPS, TOKENS], U32, name="x_codes", align_bytes=64)
        x_scales = keep.tile([P, GROUPS, TOKENS], U8, name="x_scales", align_bytes=64)
        quantise_x(nc, keep, psum, x_sb, identity, x_codes, x_scales)
        cos_pairs, sin_pairs = build_rope_tables(nc, keep)

        gate_rows = slice(32, 32 + 2)
        gate_tile = w_ring.tile([P, TILE_W_BYTES], U8, name="w", align_bytes=64)
        nc.vector.tensor_copy(
            out=gate_tile[gate_rows, 0:4].bitcast(I32), in_=planes[len(planes) - 1][gate_rows, 0, 0:4].bitcast(I32)
        )
        for t in range(LOOKAHEAD):
            fetch_tile()

        acc = [psum.tile([P, BANK_COLS], F32, name="acc%d" % bank, tag="bank%d" % bank) for bank in range(BANKS)]
        out_sb = keep.tile([P, N_OUT], F32, name="out_sb")

        def mx_pass(bank, g, w_cols):
            nc.tensor.matmul_mx(
                out=acc[bank][:],
                lhsT=x_codes[:, g, :].bitcast(FP8X4),
                lhsT_scale=x_scales[:, g, :],
                rhs=w_cols.bitcast(FP4X4),
                rhs_scale=plane(g, bank),
                start=(g == 0),
                stop=(g == GROUPS - 1),
            )

        def rope(bank):
            cols = slice(bank * BANK_COLS, (bank + 1) * BANK_COLS)
            q = acc[bank][:].rearrange("p (h d) -> p h d", h=HEADS_PER_BANK)
            q_pairs = q[:, :, NOPE_DIM:].rearrange("p h (i e) -> p h i e", e=2)
            result = out_sb[:, cols].rearrange("p (h d) -> p h d", h=HEADS_PER_BANK)
            by_cos = work.tile([P, HEADS_PER_BANK, PAIRS, 2], F32, name="by_cos")
            by_sin = work.tile([P, HEADS_PER_BANK, PAIRS, 2], F32, name="by_sin")
            for product, pairs, table in ((by_cos, q_pairs, cos_pairs), (by_sin, q_pairs[:, :, :, ::-1], sin_pairs)):
                nc.vector.tensor_tensor(
                    out=product[:],
                    in0=pairs,
                    in1=table[:].unsqueeze(1).to_broadcast([P, HEADS_PER_BANK, PAIRS, 2]),
                    op=ALU.mult,
                )
            nc.scalar.copy(out=result[:, :, :NOPE_DIM], in_=q[:, :, :NOPE_DIM])
            adder = nc.vector if bank == BANKS - 1 else nc.gpsimd
            adder.tensor_tensor(
                out=result[:, :, NOPE_DIM:].rearrange("p h (i e) -> p h i e", e=2),
                in0=by_cos[:],
                in1=by_sin[:],
                op=ALU.add,
            )

        for g in range(WORDS_FIRST):
            for bank in range(BANKS):
                mx_pass(bank, g, first_w[g][:, bank * BANK_W_BYTES : (bank + 1) * BANK_W_BYTES])

        finished = 0
        for t in range(len(TILES)):
            if len(tiles) < len(TILES):
                fetch_tile()
            first_bank, bank_end, first_group, group_end = TILES[t]
            row_bytes = (bank_end - first_bank) * BANK_W_BYTES
            for bank in range(first_bank, bank_end):
                for g in range(first_group, group_end):
                    start = (g - first_group) * row_bytes + (bank - first_bank) * BANK_W_BYTES
                    mx_pass(bank, g, tiles[t][:, start : start + BANK_W_BYTES])
                if group_end == GROUPS:
                    rope(bank)
                    finished = finished + 1
                    for store_bank, store_end in STORES:
                        if store_end == finished:
                            cols = slice(store_bank * BANK_COLS, store_end * BANK_COLS)
                            nc.sync.dma_start(out=out_rows[:, cols], in_=out_sb[:, cols])
